import numpy as np
import ml_dtypes


def mxq(x, axis, fmt="e4m3"):
    dtype, down = {"e4m3": (ml_dtypes.float8_e4m3fn, 7), "e5m2": (ml_dtypes.float8_e5m2, 14)}[fmt]
    v = np.moveaxis(np.asarray(x, np.float32).astype(ml_dtypes.bfloat16).astype(np.float64), axis, -1)
    blocks = v.reshape(v.shape[:-1] + (-1, 32))
    amax = np.abs(blocks).max(-1, keepdims=True)
    byte = np.maximum(np.where(amax > 0, np.frexp(amax)[1] - 1 + 127, 0) - down, 1)
    scale = np.exp2(byte - 127.0)
    codes = (blocks / scale).astype(np.float32).astype(dtype).astype(np.float64)
    return np.moveaxis((codes * scale).reshape(v.shape), -1, axis)


WIDE = False


def mx_kscale(k):
    if not WIDE:
        return np.ones(k)
    levels = np.array([10, -10, 5, -5, 0])
    if k % 512:
        return np.exp2(np.random.permutation(np.resize(levels, k // 32))).repeat(32)
    a = np.empty((k // 512, 16))
    for p in range(k // 512):
        a[p, :8] = np.random.permutation(np.resize(levels, 8))
        for g in range(8):
            far = levels[np.abs(levels - a[p, g]) >= 10]
            a[p, g + 8] = far[np.random.randint(len(far))]
    return np.exp2(a.ravel()).repeat(32)


BF16 = ml_dtypes.bfloat16


def bf(x):
    return np.asarray(x, np.float32).astype(BF16)


def f64(x):
    return np.asarray(x).astype(np.float64)


B, S, D, NH = 2, 512, 1024, 8
SCALE = np.sqrt(D // NH)


def draw0():
    s, t = mx_kscale(D), mx_kscale(D)
    return {"x": bf(np.random.standard_normal((B, S, D)) * s),
            "wq": bf(np.random.standard_normal((D, D)) * 0.84 / np.sqrt(D) / s[None, :] * t[:, None]),
            "wk": bf(np.random.standard_normal((D, D)) * 0.84 / np.sqrt(D) / s[None, :] / t[:, None])}


def core(x, wq, wk):
    xq = mxq(f64(x), 2, "e4m3")
    q = xq @ mxq(f64(wq), 1, "e4m3").T
    k = xq @ mxq(f64(wk), 1, "e4m3").T
    sc = (mxq(q, 2, "e4m3") @ mxq(k, 2, "e4m3").transpose(0, 2, 1)) / SCALE
    e = np.exp(sc - sc.max(-1, keepdims=True))
    return e / e.sum(-1, keepdims=True)


def e4m3fn_bytes(y):
    return np.clip(np.asarray(y, np.float64), -448.0, 448.0).astype(np.float32).astype(ml_dtypes.float8_e4m3fn).view(np.uint8)


def e4m3fn_values(b):
    return np.asarray(b, np.uint8).view(ml_dtypes.float8_e4m3fn).astype(np.float64)


def setup_inputs():
    d = draw0()
    x0 = np.asarray(d['x']).astype(np.float64)
    s = (np.max(np.abs(x0), axis=(0, 1), keepdims=True) / 448.0).astype(np.float32)
    out = {}
    for k, v in d.items():
        if k == 'x':
            out['x_bytes'] = e4m3fn_bytes(x0 / s.astype(np.float64))
            out['x_scale'] = s
        else:
            out[k] = v
    return out


def reference(x_bytes, x_scale, wq, wk):
    return core(e4m3fn_values(x_bytes) * x_scale.astype(np.float64), wq, wk)

@@ -1,0 +1,299 @@
+from contextlib import ExitStack
+
+import concourse.mybir as mybir
+from concourse.masks import make_identity
+
+B, S, D = 2, 512, 1024
+SCALE = 128.0 ** -0.5
+FLOPS = 2 * 2 * B * S * D * D + 2 * B * S * S * D
+
+F32 = mybir.dt.float32
+BF16 = mybir.dt.bfloat16
+U32 = mybir.dt.uint32
+U8 = mybir.dt.uint8
+FP8 = mybir.dt.float8_e4m3fn
+FP8X4 = mybir.dt.float8_e4m3fn_x4
+ALU = mybir.AluOpType
+ACT = mybir.ActivationFunctionType
+
+P = 128
+G = 2
+T = 4
+J = 4
+F = 2
+
+
+def tile_attentionnet_pa_kernel(tc, x_bytes, x_scale, wq, wk, out):
+    nc = tc.nc
+    with ExitStack() as ctx:
+        keep = ctx.enter_context(tc.tile_pool(name="keep", bufs=1))
+        wgrp = ctx.enter_context(tc.tile_pool(name="wgrp", bufs=2))
+        stage = ctx.enter_context(tc.tile_pool(name="stage", bufs=3))
+        soft = ctx.enter_context(tc.tile_pool(name="soft", bufs=4))
+        psum = ctx.enter_context(tc.psum_pool(name="psum", bufs=8))
+
+        xs = keep.tile([P, G, 2, 2], F32, name="xs")
+        nc.sync.dma_start(out=xs[:].rearrange("p g u e -> p g (u e)"), in_=x_scale.rearrange("o i (g p t) -> p (o i g) t", g=G, t=T))
+        xraw = [keep.tile([P, J, D], U8, name=f"xraw{b}") for b in range(B)]
+        wraw = {}
+        for m in range(2):
+            for f in range(F):
+                wraw[m, f] = keep.tile([P, T, D], BF16, name=f"wraw{m}{f}", align_bytes=64)
+
+        def load_x(b):
+            nc.sync.dma_start(out=xraw[b][:], in_=x_bytes[b].rearrange("(r j) k -> r j k", j=J))
+
+        def load_w(m, f):
+            rows = (wk, wq)[m][f * 512:(f + 1) * 512, :].rearrange("(m t) k -> m t k", t=T)
+            for h in range(2):
+                nc.sync.dma_start(out=wraw[m, f][:, 2 * h:2 * h + 2, :], in_=rows[:, 2 * h:2 * h + 2, :])
+
+        load_x(0)
+        load_w(0, 0)
+        load_w(0, 1)
+        load_w(1, 0)
+        load_x(1)
+        load_w(1, 1)
+
+        ident = keep.tile([P, P], F32, name="ident")
+        make_identity(nc, ident[:])
+        warm = keep.tile([P, 1], F32, name="warm")
+        nc.vector.memset(warm[:], 0.0)
+        nc.scalar.activation(out=warm[:], in_=warm[:], func=ACT.Exp)
+        one = keep.tile([P, 1], F32, name="one")
+        nc.vector.memset(one[:], 1.0)
+
+        xw, xg = {}, {}
+        xc, xp = {}, {}
+        for b in range(B):
+            xc[b] = keep.tile([P, J, G, P], U32, name=f"xc{b}", align_bytes=64)
+            xp[b] = keep.tile([P, J, G, P], U8, name=f"xp{b}", align_bytes=64)
+        wc, wp = {}, {}
+        for m in range(2):
+            for f in range(F):
+                wc[m, f] = keep.tile([P, T, G, P], U32, name=f"wc{m}{f}", align_bytes=64)
+                wp[m, f] = keep.tile([P, T, G, P], U8, name=f"wp{m}{f}", align_bytes=64)
+        kc, kp = {}, {}
+        for b in range(B):
+            kc[b] = keep.tile([P, F, J, P], U32, name=f"kc{b}", align_bytes=64)
+            kp[b] = keep.tile([P, F, J, P], U8, name=f"kp{b}", align_bytes=64)
+
+        def transposes(views):
+            bank = psum.tile([P, G, 2, P], F32, name="bank", tag="bank")
+            for g in range(G):
+                for u in range(2):
+                    nc.tensor.transpose(bank[:, g, u, :], views[g][u], ident[:])
+            return bank
+
+        def widen(b, j):
+            t = stage.tile([P, G, 2, P, 2], BF16, name="xwide", tag="xwide", bufs=4, align_bytes=64)
+            for g in range(G):
+                nc.vector.tensor_scalar(out=t[:, g].rearrange("r u p e -> r p u e"),
+                                        in0=xraw[b][:, j, g * 512:(g + 1) * 512].bitcast(FP8).rearrange("r (p u e) -> r p u e", u=2, e=2),
+                                        scalar1=one[:], scalar2=None, op0=ALU.mult)
+            xw[b, j] = t
+
+        xbank = {}
+
+        def x_turn(b, j):
+            t = xw[b, j]
+            xbank[b, j] = transposes([[t[:, g, u].rearrange("r p e -> r (p e)").bitcast(F32) for u in range(2)] for g in range(G)])
+
+        def x_scale_out(b, j):
+            bank = xbank[b, j]
+            grp = stage.tile([P, G, P, T], BF16, name="xgrp", tag="xgrp", bufs=4, align_bytes=64)
+            for g in range(G):
+                nc.vector.tensor_tensor(
+                    out=grp[:, g].rearrange("p r (u e) -> p r u e", u=2),
+                    in0=bank[:, g].bitcast(BF16).rearrange("p u (r e) -> p r u e", e=2),
+                    in1=xs[:, g].unsqueeze(1).to_broadcast([P, P, 2, 2]),
+                    op=ALU.mult)
+            xg[b, j] = grp
+
+        def x_quant(b, j):
+            grp = xg[b, j]
+            nc.vector.quantize_mx(
+                out=xc[b][:, j].rearrange("p g r -> p (g r)").bitcast(FP8X4),
+                scales=xp[b][:, j].rearrange("p g r -> p (g r)"),
+                in_=grp[:].rearrange("p g r t -> p (g r t)"))
+
+        wg = {}
+
+        def w_slot(m, f, s):
+            if s == 0:
+                wg[m, f] = wgrp.tile([P, T, G, P, T], BF16, name="wgrp_t", tag="wgrp_t", align_bytes=64)
+            words = wraw[m, f][:, s, :].bitcast(F32)
+            bank = transposes([[words[:, 256 * g + u:256 * (g + 1):2] for u in range(2)] for g in range(G)])
+            nc.scalar.copy(out=wg[m, f][:, s].bitcast(F32), in_=bank[:].rearrange("p g u r -> p g r u"))
+
+        def w_quant(m, f, h):
+                sl = slice(2 * h, 2 * h + 2)
+                nc.vector.quantize_mx(
+                    out=wc[m, f][:, sl].rearrange("p s g r -> p (s g r)").bitcast(FP8X4),
+                    scales=wp[m, f][:, sl].rearrange("p s g r -> p (s g r)"),
+                    in_=wg[m, f][:, sl].rearrange("p s g r t -> p (s g r t)"))
+
+        def project(m, f, b, j, dst):
+            bank = psum.tile([P, T, P], F32, name="bank", tag="bank")
+            for t in range(T):
+                for g in range(G):
+                    nc.tensor.matmul_mx(
+                        out=bank[:, t, :],
+                        lhsT=wc[m, f][:, t, g, :].bitcast(FP8X4), lhsT_scale=wp[m, f][:, t, g, :],
+                        rhs=xc[b][:, j, g, :].bitcast(FP8X4), rhs_scale=xp[b][:, j, g, :],
+                        start=(g == 0), stop=(g == G - 1))
+            nc.scalar.copy(out=dst, in_=bank[:].rearrange("p t n -> p n t"))
+
+        kg = {}
+
+        def k_proj(b, f, j):
+            if j % 2 == 0:
+                kg[b, f, j // 2] = stage.tile([P, 2, P, T], BF16, name="kgrp", tag="kgrp", bufs=4, align_bytes=64)
+            project(0, f, b, j, kg[b, f, j // 2][:, j % 2])
+
+        def k_quant(b, f, h):
+            sl = slice(2 * h, 2 * h + 2)
+            nc.vector.quantize_mx(
+                out=kc[b][:, f, sl].rearrange("p j r -> p (j r)").bitcast(FP8X4),
+                scales=kp[b][:, f, sl].rearrange("p j r -> p (j r)"),
+                in_=kg[b, f, h][:].rearrange("p j r t -> p (j r t)"))
+
+        qc, qg = {}, {}
+        sbank, top, nbias, e, tot, inv = {}, {}, {}, {}, {}, {}
+
+        def q_proj(b, f, j):
+            if (b, j) not in qg:
+                qg[b, j] = stage.tile([P, F, P, T], BF16, name="qgrp", tag="qgrp", bufs=5, align_bytes=64)
+            project(1, f, b, j, qg[b, j][:, f])
+
+        def q_quant(b, j):
+            grp = qg[b, j]
+            c = stage.tile([P, F, P], U32, name="qcode", tag="qcode", bufs=6, align_bytes=64)
+            p = stage.tile([P, F, P], U8, name="qplane", tag="qplane", bufs=6, align_bytes=64)
+            nc.vector.quantize_mx(
+                out=c[:].rearrange("p f r -> p (f r)").bitcast(FP8X4),
+                scales=p[:].rearrange("p f r -> p (f r)"),
+                in_=grp[:].rearrange("p f r t -> p (f r t)"))
+            qc[b, j] = (c, p)
+
+        def scores(b, j):
+            c, p = qc[b, j]
+            bank = psum.tile([P, J, P], F32, name="bank", tag="bank")
+            for f in range(F):
+                nc.tensor.matmul_mx(
+                    out=bank[:].rearrange("p j r -> p (j r)"),
+                    lhsT=c[:, f, :].bitcast(FP8X4), lhsT_scale=p[:, f, :],
+                    rhs=kc[b][:, f].rearrange("p j r -> p (j r)").bitcast(FP8X4),
+                    rhs_scale=kp[b][:, f].rearrange("p j r -> p (j r)"),
+                    start=(f == 0), stop=(f == F - 1))
+            sbank[b, j] = bank
+
+        def row_max(b, j):
+            top[b, j] = soft.tile([P, 1], F32, name="top")
+            nc.vector.tensor_reduce(out=top[b, j][:], in_=sbank[b, j][:].rearrange("p j r -> p (j r)"), axis=mybir.AxisListType.X, op=ALU.max)
+
+        def row_bias(b, j):
+            nbias[b, j] = soft.tile([P, 1], F32, name="nbias")
+            nc.vector.tensor_scalar(out=nbias[b, j][:], in0=top[b, j][:], scalar1=-SCALE, scalar2=None, op0=ALU.mult)
+
+        def row_exp(b, j):
+            e[b, j] = soft.tile([P, P, J], F32, name="e")
+            tot[b, j] = soft.tile([P, 1], F32, name="tot")
+            nc.scalar.activation(out=e[b, j][:], in_=sbank[b, j][:].rearrange("p j r -> p r j"), func=ACT.Exp,
+                                 bias=nbias[b, j][:], scale=SCALE, accum_out=tot[b, j][:])
+
+        def row_inv(b, j):
+            inv[b, j] = soft.tile([P, 1], F32, name="inv")
+            nc.vector.reciprocal(out=inv[b, j][:], in_=tot[b, j][:])
+
+        def row_out(b, j):
+            o = soft.tile([P, S], F32, name="o")
+            nc.vector.tensor_scalar(out=o[:], in0=e[b, j][:].rearrange("p r j -> p (r j)"), scalar1=inv[b, j][:], scalar2=None, op0=ALU.mult)
+            nc.sync.dma_start(out=out[b].rearrange("(r j) s -> r j s", j=J)[:, j, :], in_=o[:])
+
+        ctx.enter_context(tc.manual_schedule())
+        for j in range(J):
+            widen(0, j)
+        x_turn(0, 0)
+        w_slot(0, 0, 0)
+        w_slot(0, 0, 1)
+        x_turn(0, 1)
+        x_scale_out(0, 0)
+        w_quant(0, 0, 0)
+        x_scale_out(0, 1)
+        w_slot(0, 0, 2)
+        w_slot(0, 0, 3)
+        x_turn(0, 2)
+        x_quant(0, 0)
+        x_quant(0, 1)
+        x_scale_out(0, 2)
+        w_quant(0, 0, 1)
+        x_turn(0, 3)
+        x_scale_out(0, 3)
+        x_quant(0, 2)
+        x_quant(0, 3)
+        for s in range(T):
+            w_slot(0, 1, s)
+        w_quant(0, 1, 0)
+        w_quant(0, 1, 1)
+        for j in range(J):
+            k_proj(0, 0, j)
+        widen(1, 0)
+        widen(1, 1)
+        k_quant(0, 0, 0)
+        k_quant(0, 0, 1)
+        for s in range(T):
+            w_slot(1, 0, s)
+        w_quant(1, 0, 0)
+        w_quant(1, 0, 1)
+        for j in range(J):
+            k_proj(0, 1, j)
+        k_quant(0, 1, 0)
+        k_quant(0, 1, 1)
+        x_turn(1, 0)
+        x_turn(1, 1)
+        x_scale_out(1, 0)
+        widen(1, 2)
+        x_scale_out(1, 1)
+        widen(1, 3)
+        for s in range(T):
+            w_slot(1, 1, s)
+        w_quant(1, 1, 0)
+        w_quant(1, 1, 1)
+        for j in range(J):
+            q_proj(0, 0, j)
+        x_quant(1, 0)
+        x_quant(1, 1)
+        x_turn(1, 2)
+        x_turn(1, 3)
+        x_scale_out(1, 2)
+        x_scale_out(1, 3)
+        for j in range(J):
+            q_proj(0, 1, j)
+            q_quant(0, j)
+        x_quant(1, 2)
+        x_quant(1, 3)
+        tiles = [(b, j) for b in range(B) for j in range(J)]
+        for i in range(len(tiles) + 4):
+            if 0 <= i - 4 < 8:
+                row_inv(*tiles[i - 4])
+            if i < 4:
+                k_proj(1, 0, i)
+                k_proj(1, 1, i)
+            elif i < 8:
+                q_proj(1, 0, i - 4)
+                q_proj(1, 1, i - 4)
+            if 0 <= i - 2 < 8:
+                scores(*tiles[i - 2])
+                row_max(*tiles[i - 2])
+            if i < 4 and i % 2:
+                k_quant(1, 0, i // 2)
+                k_quant(1, 1, i // 2)
+            if 4 <= i < 8:
+                q_quant(1, i - 4)
+            if 0 <= i - 2 < 8:
+                row_bias(*tiles[i - 2])
+            if 0 <= i - 3 < 8:
+                row_exp(*tiles[i - 3])
+            if 0 <= i - 4 < 8:
+                row_out(*tiles[i - 4])

@@ -33,33 +33,41 @@ def tile_attentionnet_pa_kernel(tc, x_bytes, x_scale, wq, wk, out):
         psum = ctx.enter_context(tc.psum_pool(name="psum", bufs=8))
 
         xs = keep.tile([P, G, 2, 2], F32, name="xs")
-        nc.sync.dma_start(out=xs[:].rearrange("p g u e -> p g (u e)"), in_=x_scale.rearrange("o i (g p t) -> p (o i g) t", g=G, t=T))
         xraw = [keep.tile([P, J, D], U8, name=f"xraw{b}") for b in range(B)]
         wraw = {}
         for m in range(2):
             for f in range(F):
                 wraw[m, f] = keep.tile([P, T, D], BF16, name=f"wraw{m}{f}", align_bytes=64)
 
-        def load_x(b):
-            nc.sync.dma_start(out=xraw[b][:], in_=x_bytes[b].rearrange("(r j) k -> r j k", j=J))
+        def load_x(b, js):
+            nc.sync.dma_start(out=xraw[b][:, js, :], in_=x_bytes[b].rearrange("(r j) k -> r j k", j=J)[:, js, :])
 
-        def load_w(m, f):
+        def load_xs():
+            nc.sync.dma_start(out=xs[:].rearrange("p g u e -> p g (u e)"), in_=x_scale.rearrange("o i (g p t) -> p (o i g) t", g=G, t=T))
+
+        def load_w(m, f, h):
             rows = (wk, wq)[m][f * 512:(f + 1) * 512, :].rearrange("(m t) k -> m t k", t=T)
-            for h in range(2):
-                nc.sync.dma_start(out=wraw[m, f][:, 2 * h:2 * h + 2, :], in_=rows[:, 2 * h:2 * h + 2, :])
+            nc.sync.dma_start(out=wraw[m, f][:, 2 * h:2 * h + 2, :], in_=rows[:, 2 * h:2 * h + 2, :])
 
-        load_x(0)
-        load_w(0, 0)
-        load_w(0, 1)
-        load_w(1, 0)
-        load_x(1)
-        load_w(1, 1)
+        load_x(0, slice(0, 2))
+        load_xs()
+        load_w(0, 0, 0)
+        load_w(0, 0, 1)
+        load_x(0, slice(2, 4))
+        for m, f in ((0, 1), (1, 0)):
+            for h in range(2):
+                load_w(m, f, h)
+        load_x(1, slice(0, 4))
+        for h in range(2):
+            load_w(1, 1, h)
 
         ident = keep.tile([P, P], F32, name="ident")
         make_identity(nc, ident[:])
         warm = keep.tile([P, 1], F32, name="warm")
         nc.vector.memset(warm[:], 0.0)
         nc.scalar.activation(out=warm[:], in_=warm[:], func=ACT.Exp)
+        zero = keep.tile([P, 512], BF16, name="zero")
+        nc.vector.memset(zero[:], 0.0)
         one = keep.tile([P, 1], F32, name="one")
         nc.vector.memset(one[:], 1.0)
 
@@ -85,19 +93,26 @@ def tile_attentionnet_pa_kernel(tc, x_bytes, x_scale, wq, wk, out):
                     nc.tensor.transpose(bank[:, g, u, :], views[g][u], ident[:])
             return bank
 
-        def widen(b, j):
+        def widen_v(b, j):
             t = stage.tile([P, G, 2, P, 2], BF16, name="xwide", tag="xwide", bufs=4, align_bytes=64)
             for g in range(G):
                 nc.vector.tensor_scalar(out=t[:, g].rearrange("r u p e -> r p u e"),
                                         in0=xraw[b][:, j, g * 512:(g + 1) * 512].bitcast(FP8).rearrange("r (p u e) -> r p u e", u=2, e=2),
                                         scalar1=one[:], scalar2=None, op0=ALU.mult)
-            xw[b, j] = t
+            xw[b, j] = [[t[:, g, u].rearrange("r p e -> r (p e)").bitcast(F32) for u in range(2)] for g in range(G)]
+
+        def every_second(words):
+            return [[words[:, 256 * g + u:256 * (g + 1):2] for u in range(2)] for g in range(G)]
+
+        def widen_s(b, j):
+            t = stage.tile([P, D], BF16, name="xwide", tag="xwide", bufs=4, align_bytes=64)
+            nc.scalar.copy(out=t[:], in_=xraw[b][:, j, :].bitcast(FP8))
+            xw[b, j] = every_second(t[:].bitcast(F32))
 
         xbank = {}
 
         def x_turn(b, j):
-            t = xw[b, j]
-            xbank[b, j] = transposes([[t[:, g, u].rearrange("r p e -> r (p e)").bitcast(F32) for u in range(2)] for g in range(G)])
+            xbank[b, j] = transposes(xw[b, j])
 
         def x_scale_out(b, j):
             bank = xbank[b, j]
@@ -122,8 +137,7 @@ def tile_attentionnet_pa_kernel(tc, x_bytes, x_scale, wq, wk, out):
         def w_slot(m, f, s):
             if s == 0:
                 wg[m, f] = wgrp.tile([P, T, G, P, T], BF16, name="wgrp_t", tag="wgrp_t", align_bytes=64)
-            words = wraw[m, f][:, s, :].bitcast(F32)
-            bank = transposes([[words[:, 256 * g + u:256 * (g + 1):2] for u in range(2)] for g in range(G)])
+            bank = transposes(every_second(wraw[m, f][:, s, :].bitcast(F32)))
             nc.scalar.copy(out=wg[m, f][:, s].bitcast(F32), in_=bank[:].rearrange("p g u r -> p g r u"))
 
         def w_quant(m, f, h):
@@ -133,7 +147,7 @@ def tile_attentionnet_pa_kernel(tc, x_bytes, x_scale, wq, wk, out):
                     scales=wp[m, f][:, sl].rearrange("p s g r -> p (s g r)"),
                     in_=wg[m, f][:, sl].rearrange("p s g r t -> p (s g r t)"))
 
-        def project(m, f, b, j, dst):
+        def project(m, f, b, j, dst, vector):
             bank = psum.tile([P, T, P], F32, name="bank", tag="bank")
             for t in range(T):
                 for g in range(G):
@@ -142,14 +156,17 @@ def tile_attentionnet_pa_kernel(tc, x_bytes, x_scale, wq, wk, out):
                         lhsT=wc[m, f][:, t, g, :].bitcast(FP8X4), lhsT_scale=wp[m, f][:, t, g, :],
                         rhs=xc[b][:, j, g, :].bitcast(FP8X4), rhs_scale=xp[b][:, j, g, :],
                         start=(g == 0), stop=(g == G - 1))
-            nc.scalar.copy(out=dst, in_=bank[:].rearrange("p t n -> p n t"))
+            if vector:
+                nc.vector.tensor_copy(out=dst, in_=bank[:].rearrange("p t n -> p n t"))
+            else:
+                nc.scalar.copy(out=dst, in_=bank[:].rearrange("p t n -> p n t"))
 
         kg = {}
 
-        def k_proj(b, f, j):
+        def k_proj(b, f, j, vector=False):
             if j % 2 == 0:
                 kg[b, f, j // 2] = stage.tile([P, 2, P, T], BF16, name="kgrp", tag="kgrp", bufs=4, align_bytes=64)
-            project(0, f, b, j, kg[b, f, j // 2][:, j % 2])
+            project(0, f, b, j, kg[b, f, j // 2][:, j % 2], vector)
 
         def k_quant(b, f, h):
             sl = slice(2 * h, 2 * h + 2)
@@ -159,12 +176,12 @@ def tile_attentionnet_pa_kernel(tc, x_bytes, x_scale, wq, wk, out):
                 in_=kg[b, f, h][:].rearrange("p j r t -> p (j r t)"))
 
         qc, qg = {}, {}
-        sbank, top, nbias, e, tot, inv = {}, {}, {}, {}, {}, {}
+        sbank, nbias, e, tot, inv = {}, {}, {}, {}, {}
 
-        def q_proj(b, f, j):
+        def q_proj(b, f, j, vector=False):
             if (b, j) not in qg:
                 qg[b, j] = stage.tile([P, F, P, T], BF16, name="qgrp", tag="qgrp", bufs=5, align_bytes=64)
-            project(1, f, b, j, qg[b, j][:, f])
+            project(1, f, b, j, qg[b, j][:, f], vector)
 
         def q_quant(b, j):
             grp = qg[b, j]
@@ -188,13 +205,11 @@ def tile_attentionnet_pa_kernel(tc, x_bytes, x_scale, wq, wk, out):
                     start=(f == 0), stop=(f == F - 1))
             sbank[b, j] = bank
 
-        def row_max(b, j):
-            top[b, j] = soft.tile([P, 1], F32, name="top")
-            nc.vector.tensor_reduce(out=top[b, j][:], in_=sbank[b, j][:].rearrange("p j r -> p (j r)"), axis=mybir.AxisListType.X, op=ALU.max)
-
         def row_bias(b, j):
             nbias[b, j] = soft.tile([P, 1], F32, name="nbias")
-            nc.vector.tensor_scalar(out=nbias[b, j][:], in0=top[b, j][:], scalar1=-SCALE, scalar2=None, op0=ALU.mult)
+            scratch = soft.tile([P, S], F32, name="scratch")
+            nc.vector.tensor_scalar(out=scratch[:], in0=sbank[b, j][:].rearrange("p j r -> p (j r)"), scalar1=-SCALE, scalar2=None,
+                                    op0=ALU.mult, op1=ALU.min, accum_out=nbias[b, j][:])
 
         def row_exp(b, j):
             e[b, j] = soft.tile([P, P, J], F32, name="e")
@@ -212,88 +227,120 @@ def tile_attentionnet_pa_kernel(tc, x_bytes, x_scale, wq, wk, out):
             nc.sync.dma_start(out=out[b].rearrange("(r j) s -> r j s", j=J)[:, j, :], in_=o[:])
 
         ctx.enter_context(tc.manual_schedule())
-        for j in range(J):
-            widen(0, j)
+        def dummy():
+            bank = psum.tile([P, 512], F32, name="bank", tag="bank")
+            nc.tensor.matmul(bank[:], lhsT=zero[:, 0:P], rhs=zero[:], start=True, stop=True)
+
+        def w_slots(m, f, *ss):
+            for s in ss:
+                w_slot(m, f, s)
+
+        for i in range(5):
+            dummy()
+        widen_v(0, 0)
+        widen_s(0, 1)
         x_turn(0, 0)
-        w_slot(0, 0, 0)
-        w_slot(0, 0, 1)
-        x_turn(0, 1)
+        w_slots(0, 0, 0)
+        dummy()
+        w_slots(0, 0, 1)
         x_scale_out(0, 0)
-        w_quant(0, 0, 0)
-        x_scale_out(0, 1)
-        w_slot(0, 0, 2)
-        w_slot(0, 0, 3)
-        x_turn(0, 2)
+        x_turn(0, 1)
+        dummy()
         x_quant(0, 0)
+        x_scale_out(0, 1)
+        widen_s(0, 2)
+        w_slots(0, 0, 2, 3)
+        dummy()
+        w_quant(0, 0, 0)
         x_quant(0, 1)
-        x_scale_out(0, 2)
+        widen_s(0, 3)
+        w_slots(0, 1, 0)
+        x_turn(0, 2)
+        dummy()
         w_quant(0, 0, 1)
+        x_scale_out(0, 2)
+        w_slots(0, 1, 1, 2)
+        dummy()
+        w_slots(0, 1, 3)
         x_turn(0, 3)
+        dummy()
         x_scale_out(0, 3)
         x_quant(0, 2)
         x_quant(0, 3)
-        for s in range(T):
-            w_slot(0, 1, s)
+        w_slots(1, 0, 0)
         w_quant(0, 1, 0)
         w_quant(0, 1, 1)
         for j in range(J):
             k_proj(0, 0, j)
-        widen(1, 0)
-        widen(1, 1)
+        widen_v(1, 0)
         k_quant(0, 0, 0)
+        widen_v(1, 1)
         k_quant(0, 0, 1)
-        for s in range(T):
-            w_slot(1, 0, s)
+        w_slots(1, 0, 1, 2, 3)
+        x_turn(1, 0)
         w_quant(1, 0, 0)
+        widen_v(1, 2)
         w_quant(1, 0, 1)
+        widen_v(1, 3)
         for j in range(J):
             k_proj(0, 1, j)
         k_quant(0, 1, 0)
-        k_quant(0, 1, 1)
-        x_turn(1, 0)
-        x_turn(1, 1)
         x_scale_out(1, 0)
-        widen(1, 2)
+        k_quant(0, 1, 1)
+        w_slots(1, 1, 0)
+        x_turn(1, 1)
         x_scale_out(1, 1)
-        widen(1, 3)
-        for s in range(T):
-            w_slot(1, 1, s)
-        w_quant(1, 1, 0)
-        w_quant(1, 1, 1)
-        for j in range(J):
-            q_proj(0, 0, j)
         x_quant(1, 0)
         x_quant(1, 1)
+        w_slots(1, 1, 1, 2, 3)
         x_turn(1, 2)
         x_turn(1, 3)
+        w_quant(1, 1, 0)
+        w_quant(1, 1, 1)
         x_scale_out(1, 2)
         x_scale_out(1, 3)
-        for j in range(J):
-            q_proj(0, 1, j)
-            q_quant(0, j)
         x_quant(1, 2)
         x_quant(1, 3)
-        tiles = [(b, j) for b in range(B) for j in range(J)]
-        for i in range(len(tiles) + 4):
-            if 0 <= i - 4 < 8:
-                row_inv(*tiles[i - 4])
-            if i < 4:
-                k_proj(1, 0, i)
-                k_proj(1, 1, i)
-            elif i < 8:
-                q_proj(1, 0, i - 4)
-                q_proj(1, 1, i - 4)
-            if 0 <= i - 2 < 8:
-                scores(*tiles[i - 2])
-                row_max(*tiles[i - 2])
+        for f in range(F):
+            for j in range(J):
+                q_proj(0, f, j)
+        for j in range(J):
+            q_quant(0, j)
+        due = {}
+        for j in range(J):
+            due[j + 1] = (0, j)
+            due[j + 6] = (1, j)
+        for i in range(8):
+            j = i % 4
+            now, prev = due.get(i), due.get(i - 1)
+            proj = k_proj if i < 4 else q_proj
+            proj(1, 0, j)
+            if prev:
+                row_exp(*prev)
+            proj(1, 1, j, i in (1, 3, 5))
             if i < 4 and i % 2:
                 k_quant(1, 0, i // 2)
                 k_quant(1, 1, i // 2)
-            if 4 <= i < 8:
-                q_quant(1, i - 4)
-            if 0 <= i - 2 < 8:
-                row_bias(*tiles[i - 2])
-            if 0 <= i - 3 < 8:
-                row_exp(*tiles[i - 3])
-            if 0 <= i - 4 < 8:
-                row_out(*tiles[i - 4])
+            if now:
+                scores(*now)
+            if prev:
+                row_inv(*prev)
+            if now:
+                row_bias(*now)
+            if i >= 4:
+                q_quant(1, j)
+            if prev:
+                row_out(*prev)
+        scores(1, 2)
+        scores(1, 3)
+        row_exp(1, 1)
+        row_bias(1, 2)
+        row_exp(1, 2)
+        row_inv(1, 1)
+        row_bias(1, 3)
+        row_exp(1, 3)
+        row_out(1, 1)
+        row_inv(1, 2)
+        row_out(1, 2)
+        row_inv(1, 3)
+        row_out(1, 3)

from contextlib import ExitStack

import concourse.mybir as mybir
from concourse.masks import make_identity

B, S, D = 2, 512, 1024
SCALE = 128.0 ** -0.5
FLOPS = 2 * 2 * B * S * D * D + 2 * B * S * S * D

F32 = mybir.dt.float32
BF16 = mybir.dt.bfloat16
U32 = mybir.dt.uint32
U8 = mybir.dt.uint8
FP8 = mybir.dt.float8_e4m3fn
FP8X4 = mybir.dt.float8_e4m3fn_x4
ALU = mybir.AluOpType
ACT = mybir.ActivationFunctionType

P = 128
G = 2
T = 4
J = 4
F = 2


def tile_attentionnet_pa_kernel(tc, x_bytes, x_scale, wq, wk, out):
    nc = tc.nc
    with ExitStack() as ctx:
        keep = ctx.enter_context(tc.tile_pool(name="keep", bufs=1))
        wgrp = ctx.enter_context(tc.tile_pool(name="wgrp", bufs=2))
        stage = ctx.enter_context(tc.tile_pool(name="stage", bufs=3))
        soft = ctx.enter_context(tc.tile_pool(name="soft", bufs=4))
        psum = ctx.enter_context(tc.psum_pool(name="psum", bufs=8))

        xs = keep.tile([P, G, 2, 2], F32, name="xs")
        xraw = [keep.tile([P, J, D], U8, name=f"xraw{b}") for b in range(B)]
        wraw = {}
        for m in range(2):
            for f in range(F):
                wraw[m, f] = keep.tile([P, T, D], BF16, name=f"wraw{m}{f}", align_bytes=64)

        def load_x(b, js):
            nc.sync.dma_start(out=xraw[b][:, js, :], in_=x_bytes[b].rearrange("(r j) k -> r j k", j=J)[:, js, :])

        def load_xs():
            nc.sync.dma_start(out=xs[:].rearrange("p g u e -> p g (u e)"), in_=x_scale.rearrange("o i (g p t) -> p (o i g) t", g=G, t=T))

        def load_w(m, f, h):
            rows = (wk, wq)[m][f * 512:(f + 1) * 512, :].rearrange("(m t) k -> m t k", t=T)
            nc.sync.dma_start(out=wraw[m, f][:, 2 * h:2 * h + 2, :], in_=rows[:, 2 * h:2 * h + 2, :])

        load_x(0, slice(0, 2))
        load_xs()
        load_w(0, 0, 0)
        load_w(0, 0, 1)
        load_x(0, slice(2, 4))
        for m, f in ((0, 1), (1, 0)):
            for h in range(2):
                load_w(m, f, h)
        load_x(1, slice(0, 4))
        for h in range(2):
            load_w(1, 1, h)

        ident = keep.tile([P, P], F32, name="ident")
        make_identity(nc, ident[:])
        warm = keep.tile([P, 1], F32, name="warm")
        nc.vector.memset(warm[:], 0.0)
        nc.scalar.activation(out=warm[:], in_=warm[:], func=ACT.Exp)
        zero = keep.tile([P, 512], BF16, name="zero")
        nc.vector.memset(zero[:], 0.0)
        one = keep.tile([P, 1], F32, name="one")
        nc.vector.memset(one[:], 1.0)

        xw, xg = {}, {}
        xc, xp = {}, {}
        for b in range(B):
            xc[b] = keep.tile([P, J, G, P], U32, name=f"xc{b}", align_bytes=64)
            xp[b] = keep.tile([P, J, G, P], U8, name=f"xp{b}", align_bytes=64)
        wc, wp = {}, {}
        for m in range(2):
            for f in range(F):
                wc[m, f] = keep.tile([P, T, G, P], U32, name=f"wc{m}{f}", align_bytes=64)
                wp[m, f] = keep.tile([P, T, G, P], U8, name=f"wp{m}{f}", align_bytes=64)
        kc, kp = {}, {}
        for b in range(B):
            kc[b] = keep.tile([P, F, J, P], U32, name=f"kc{b}", align_bytes=64)
            kp[b] = keep.tile([P, F, J, P], U8, name=f"kp{b}", align_bytes=64)

        def transposes(views):
            bank = psum.tile([P, G, 2, P], F32, name="bank", tag="bank")
            for g in range(G):
                for u in range(2):
                    nc.tensor.transpose(bank[:, g, u, :], views[g][u], ident[:])
            return bank

        def widen_v(b, j):
            t = stage.tile([P, G, 2, P, 2], BF16, name="xwide", tag="xwide", bufs=4, align_bytes=64)
            for g in range(G):
                nc.vector.tensor_scalar(out=t[:, g].rearrange("r u p e -> r p u e"),
                                        in0=xraw[b][:, j, g * 512:(g + 1) * 512].bitcast(FP8).rearrange("r (p u e) -> r p u e", u=2, e=2),
                                        scalar1=one[:], scalar2=None, op0=ALU.mult)
            xw[b, j] = [[t[:, g, u].rearrange("r p e -> r (p e)").bitcast(F32) for u in range(2)] for g in range(G)]

        def every_second(words):
            return [[words[:, 256 * g + u:256 * (g + 1):2] for u in range(2)] for g in range(G)]

        def widen_s(b, j):
            t = stage.tile([P, D], BF16, name="xwide", tag="xwide", bufs=4, align_bytes=64)
            nc.scalar.copy(out=t[:], in_=xraw[b][:, j, :].bitcast(FP8))
            xw[b, j] = every_second(t[:].bitcast(F32))

        xbank = {}

        def x_turn(b, j):
            xbank[b, j] = transposes(xw[b, j])

        def x_scale_out(b, j):
            bank = xbank[b, j]
            grp = stage.tile([P, G, P, T], BF16, name="xgrp", tag="xgrp", bufs=4, align_bytes=64)
            for g in range(G):
                nc.vector.tensor_tensor(
                    out=grp[:, g].rearrange("p r (u e) -> p r u e", u=2),
                    in0=bank[:, g].bitcast(BF16).rearrange("p u (r e) -> p r u e", e=2),
                    in1=xs[:, g].unsqueeze(1).to_broadcast([P, P, 2, 2]),
                    op=ALU.mult)
            xg[b, j] = grp

        def x_quant(b, j):
            grp = xg[b, j]
            nc.vector.quantize_mx(
                out=xc[b][:, j].rearrange("p g r -> p (g r)").bitcast(FP8X4),
                scales=xp[b][:, j].rearrange("p g r -> p (g r)"),
                in_=grp[:].rearrange("p g r t -> p (g r t)"))

        wg = {}

        def w_slot(m, f, s):
            if s == 0:
                wg[m, f] = wgrp.tile([P, T, G, P, T], BF16, name="wgrp_t", tag="wgrp_t", align_bytes=64)
            bank = transposes(every_second(wraw[m, f][:, s, :].bitcast(F32)))
            nc.scalar.copy(out=wg[m, f][:, s].bitcast(F32), in_=bank[:].rearrange("p g u r -> p g r u"))

        def w_quant(m, f, h):
                sl = slice(2 * h, 2 * h + 2)
                nc.vector.quantize_mx(
                    out=wc[m, f][:, sl].rearrange("p s g r -> p (s g r)").bitcast(FP8X4),
                    scales=wp[m, f][:, sl].rearrange("p s g r -> p (s g r)"),
                    in_=wg[m, f][:, sl].rearrange("p s g r t -> p (s g r t)"))

        def project(m, f, b, j, dst, vector):
            bank = psum.tile([P, T, P], F32, name="bank", tag="bank")
            for t in range(T):
                for g in range(G):
                    nc.tensor.matmul_mx(
                        out=bank[:, t, :],
                        lhsT=wc[m, f][:, t, g, :].bitcast(FP8X4), lhsT_scale=wp[m, f][:, t, g, :],
                        rhs=xc[b][:, j, g, :].bitcast(FP8X4), rhs_scale=xp[b][:, j, g, :],
                        start=(g == 0), stop=(g == G - 1))
            if vector:
                nc.vector.tensor_copy(out=dst, in_=bank[:].rearrange("p t n -> p n t"))
            else:
                nc.scalar.copy(out=dst, in_=bank[:].rearrange("p t n -> p n t"))

        kg = {}

        def k_proj(b, f, j, vector=False):
            if j % 2 == 0:
                kg[b, f, j // 2] = stage.tile([P, 2, P, T], BF16, name="kgrp", tag="kgrp", bufs=4, align_bytes=64)
            project(0, f, b, j, kg[b, f, j // 2][:, j % 2], vector)

        def k_quant(b, f, h):
            sl = slice(2 * h, 2 * h + 2)
            nc.vector.quantize_mx(
                out=kc[b][:, f, sl].rearrange("p j r -> p (j r)").bitcast(FP8X4),
                scales=kp[b][:, f, sl].rearrange("p j r -> p (j r)"),
                in_=kg[b, f, h][:].rearrange("p j r t -> p (j r t)"))

        qc, qg = {}, {}
        sbank, nbias, e, tot, inv = {}, {}, {}, {}, {}

        def q_proj(b, f, j, vector=False):
            if (b, j) not in qg:
                qg[b, j] = stage.tile([P, F, P, T], BF16, name="qgrp", tag="qgrp", bufs=5, align_bytes=64)
            project(1, f, b, j, qg[b, j][:, f], vector)

        def q_quant(b, j):
            grp = qg[b, j]
            c = stage.tile([P, F, P], U32, name="qcode", tag="qcode", bufs=6, align_bytes=64)
            p = stage.tile([P, F, P], U8, name="qplane", tag="qplane", bufs=6, align_bytes=64)
            nc.vector.quantize_mx(
                out=c[:].rearrange("p f r -> p (f r)").bitcast(FP8X4),
                scales=p[:].rearrange("p f r -> p (f r)"),
                in_=grp[:].rearrange("p f r t -> p (f r t)"))
            qc[b, j] = (c, p)

        def scores(b, j):
            c, p = qc[b, j]
            bank = psum.tile([P, J, P], F32, name="bank", tag="bank")
            for f in range(F):
                nc.tensor.matmul_mx(
                    out=bank[:].rearrange("p j r -> p (j r)"),
                    lhsT=c[:, f, :].bitcast(FP8X4), lhsT_scale=p[:, f, :],
                    rhs=kc[b][:, f].rearrange("p j r -> p (j r)").bitcast(FP8X4),
                    rhs_scale=kp[b][:, f].rearrange("p j r -> p (j r)"),
                    start=(f == 0), stop=(f == F - 1))
            sbank[b, j] = bank

        def row_bias(b, j):
            nbias[b, j] = soft.tile([P, 1], F32, name="nbias")
            scratch = soft.tile([P, S], F32, name="scratch")
            nc.vector.tensor_scalar(out=scratch[:], in0=sbank[b, j][:].rearrange("p j r -> p (j r)"), scalar1=-SCALE, scalar2=None,
                                    op0=ALU.mult, op1=ALU.min, accum_out=nbias[b, j][:])

        def row_exp(b, j):
            e[b, j] = soft.tile([P, P, J], F32, name="e")
            tot[b, j] = soft.tile([P, 1], F32, name="tot")
            nc.scalar.activation(out=e[b, j][:], in_=sbank[b, j][:].rearrange("p j r -> p r j"), func=ACT.Exp,
                                 bias=nbias[b, j][:], scale=SCALE, accum_out=tot[b, j][:])

        def row_inv(b, j):
            inv[b, j] = soft.tile([P, 1], F32, name="inv")
            nc.vector.reciprocal(out=inv[b, j][:], in_=tot[b, j][:])

        def row_out(b, j):
            o = soft.tile([P, S], F32, name="o")
            nc.vector.tensor_scalar(out=o[:], in0=e[b, j][:].rearrange("p r j -> p (r j)"), scalar1=inv[b, j][:], scalar2=None, op0=ALU.mult)
            nc.sync.dma_start(out=out[b].rearrange("(r j) s -> r j s", j=J)[:, j, :], in_=o[:])

        ctx.enter_context(tc.manual_schedule())
        def dummy():
            bank = psum.tile([P, 512], F32, name="bank", tag="bank")
            nc.tensor.matmul(bank[:], lhsT=zero[:, 0:P], rhs=zero[:], start=True, stop=True)

        def w_slots(m, f, *ss):
            for s in ss:
                w_slot(m, f, s)

        for i in range(5):
            dummy()
        widen_v(0, 0)
        widen_s(0, 1)
        x_turn(0, 0)
        w_slots(0, 0, 0)
        dummy()
        w_slots(0, 0, 1)
        x_scale_out(0, 0)
        x_turn(0, 1)
        dummy()
        x_quant(0, 0)
        x_scale_out(0, 1)
        widen_s(0, 2)
        w_slots(0, 0, 2, 3)
        dummy()
        w_quant(0, 0, 0)
        x_quant(0, 1)
        widen_s(0, 3)
        w_slots(0, 1, 0)
        x_turn(0, 2)
        dummy()
        w_quant(0, 0, 1)
        x_scale_out(0, 2)
        w_slots(0, 1, 1, 2)
        dummy()
        w_slots(0, 1, 3)
        x_turn(0, 3)
        dummy()
        x_scale_out(0, 3)
        x_quant(0, 2)
        x_quant(0, 3)
        w_slots(1, 0, 0)
        w_quant(0, 1, 0)
        w_quant(0, 1, 1)
        for j in range(J):
            k_proj(0, 0, j)
        widen_v(1, 0)
        k_quant(0, 0, 0)
        widen_v(1, 1)
        k_quant(0, 0, 1)
        w_slots(1, 0, 1, 2, 3)
        x_turn(1, 0)
        w_quant(1, 0, 0)
        widen_v(1, 2)
        w_quant(1, 0, 1)
        widen_v(1, 3)
        for j in range(J):
            k_proj(0, 1, j)
        k_quant(0, 1, 0)
        x_scale_out(1, 0)
        k_quant(0, 1, 1)
        w_slots(1, 1, 0)
        x_turn(1, 1)
        x_scale_out(1, 1)
        x_quant(1, 0)
        x_quant(1, 1)
        w_slots(1, 1, 1, 2, 3)
        x_turn(1, 2)
        x_turn(1, 3)
        w_quant(1, 1, 0)
        w_quant(1, 1, 1)
        x_scale_out(1, 2)
        x_scale_out(1, 3)
        x_quant(1, 2)
        x_quant(1, 3)
        for f in range(F):
            for j in range(J):
                q_proj(0, f, j)
        for j in range(J):
            q_quant(0, j)
        due = {}
        for j in range(J):
            due[j + 1] = (0, j)
            due[j + 6] = (1, j)
        for i in range(8):
            j = i % 4
            now, prev = due.get(i), due.get(i - 1)
            proj = k_proj if i < 4 else q_proj
            proj(1, 0, j)
            if prev:
                row_exp(*prev)
            proj(1, 1, j, i in (1, 3, 5))
            if i < 4 and i % 2:
                k_quant(1, 0, i // 2)
                k_quant(1, 1, i // 2)
            if now:
                scores(*now)
            if prev:
                row_inv(*prev)
            if now:
                row_bias(*now)
            if i >= 4:
                q_quant(1, j)
            if prev:
                row_out(*prev)
        scores(1, 2)
        scores(1, 3)
        row_exp(1, 1)
        row_bias(1, 2)
        row_exp(1, 2)
        row_inv(1, 1)
        row_bias(1, 3)
        row_exp(1, 3)
        row_out(1, 1)
        row_inv(1, 2)
        row_out(1, 2)
        row_inv(1, 3)
        row_out(1, 3)
